import numpy as np
import ml_dtypes


def mxq(x, axis, fmt="e4m3"):
    dtype, down = {"e4m3": (ml_dtypes.float8_e4m3fn, 7), "e5m2": (ml_dtypes.float8_e5m2, 14)}[fmt]
    v = np.moveaxis(np.asarray(x, np.float32).astype(ml_dtypes.bfloat16).astype(np.float64), axis, -1)
    blocks = v.reshape(v.shape[:-1] + (-1, 32))
    amax = np.abs(blocks).max(-1, keepdims=True)
    byte = np.maximum(np.where(amax > 0, np.frexp(amax)[1] - 1 + 127, 0) - down, 1)
    scale = np.exp2(byte - 127.0)
    codes = (blocks / scale).astype(np.float32).astype(dtype).astype(np.float64)
    return np.moveaxis((codes * scale).reshape(v.shape), -1, axis)


WIDE = False


def mx_kscale(k):
    if not WIDE:
        return np.ones(k)
    levels = np.array([10, -10, 5, -5, 0])
    a = np.random.permutation(np.resize(levels, k // 512 * 4)).reshape(k // 512, 4)
    idx = np.arange(k)
    return np.exp2(a[idx // 512, idx % 128 // 32])


BF16 = ml_dtypes.bfloat16


def bf(x):
    return np.asarray(x, np.float32).astype(BF16)


def f64(x):
    return np.asarray(x).astype(np.float64)


N, C0, H, KS, P, C, O, F, NC = 128, 1, 6, 3, 2, 512, 128, 512, 10
KK = KS * KS
OH = H - KS + 1
OP = OH // P
FC = O * OP * OP


def relu(v):
    return np.maximum(v, 0.0)


def maxpool(v):
    n, c, hh, ww = v.shape
    hp, wp = hh // P, ww // P
    return v[:, :, :hp * P, :wp * P].reshape(n, c, hp, P, wp, P).max(axis=(3, 5))


def setup_inputs():
    s = mx_kscale(C)
    t = mx_kscale(FC)
    tt = np.repeat(np.repeat(t.reshape(O, OP, OP), P, axis=1), P, axis=2)
    h = np.maximum(np.random.standard_normal((P * P, N, C, H, H)).max(0), 0.0)
    return {
        "h_pool1": bf(h * s[None, :, None, None]),
        "w2": bf(np.random.standard_normal((O, C, KK, OH, OH)) * 0.8 / np.sqrt(KK * C) / s[None, :, None, None, None] * tt[:, None, None, :, :]),
        "b2": bf(np.random.standard_normal((O, OH, OH)) * 0.3 * tt),
        "fc1_w": bf(np.random.standard_normal((FC, F)) * 0.8 / np.sqrt(FC) / t[:, None]),
        "fc1_b": bf(np.random.standard_normal(F) * 0.3),
    }


def reference(h_pool1, w2, b2, fc1_w, fc1_b):
    hq = mxq(f64(h_pool1).transpose(2, 3, 0, 1), 3, "e4m3")
    wq = mxq(f64(w2).transpose(2, 3, 4, 1, 0), 3, "e4m3")
    y = sum((hq[i:i + OH, j:j + OH] @ wq[i * KS + j]) for i in range(KS) for j in range(KS))
    y = y.transpose(2, 3, 0, 1) + f64(b2)
    g = maxpool(relu(y)).reshape(N, FC)
    return relu((mxq(g, 1, "e4m3") @ mxq(f64(fc1_w), 0, "e4m3")) + f64(fc1_b))

@@ -1,0 +1,198 @@
+from contextlib import ExitStack
+
+import concourse.mybir as mybir
+
+BF16 = mybir.dt.bfloat16
+F32 = mybir.dt.float32
+U32 = mybir.dt.uint32
+U8 = mybir.dt.uint8
+FP8X4 = mybir.dt.float8_e4m3fn_x4
+RELU = mybir.ActivationFunctionType.Relu
+
+P = 128
+PACK = 4
+BATCH = 128
+OUT_CH = 128
+SIDE_IN = 6
+KS = 3
+OFFSETS = KS * KS
+SIDE_OUT = 4
+POOL = 2
+DENSE_OUT = 512
+
+SHELF = 36
+HALF = 64
+RUN = 4
+PIECE_ROWS = 32
+RAW_ELEMS = 4608
+W2_COLS = RAW_ELEMS // (PACK * OFFSETS * SIDE_OUT * SIDE_OUT)
+H_COLS = RAW_ELEMS // (PACK * SIDE_IN * SIDE_IN)
+
+VECTOR_PIECES = 3
+SCALAR_PIECES = 2
+
+WINDOWS = [(u, v) for u in range(SIDE_OUT // POOL) for v in range(SIDE_OUT // POOL)]
+
+FLOPS = 2 * BATCH * OUT_CH * 512 * OFFSETS * SIDE_OUT * SIDE_OUT + 2 * BATCH * 512 * DENSE_OUT
+
+
+def positions_of(window):
+    u, v = window
+    return [(POOL * u + a, POOL * v + b) for a in range(POOL) for b in range(POOL)]
+
+
+def regroup(nc, piece, slab, first_row, src):
+    dst = slab[:, :, first_row : first_row + PIECE_ROWS].rearrange("p (a b) r -> p a r b", b=RUN)
+    if piece % (VECTOR_PIECES + SCALAR_PIECES) < VECTOR_PIECES:
+        nc.vector.tensor_copy(out=dst, in_=src)
+    else:
+        nc.scalar.copy(out=dst, in_=src)
+
+
+def quantise_half_operand(nc, slab, words, planes, operand, half):
+    cols = slice(half * HALF, (half + 1) * HALF)
+    nc.vector.quantize_mx(
+        out=words[:, operand, cols].bitcast(FP8X4),
+        scales=planes[:, operand, cols],
+        in_=slab[:, operand, :],
+    )
+
+
+def load_w2_half(nc, raw_pool, w2, slabs, half):
+    for s in range(HALF // W2_COLS):
+        first = half * HALF + s * W2_COLS
+        raw = raw_pool.tile([P, W2_COLS * PACK, OFFSETS * SIDE_OUT * SIDE_OUT], BF16, tag="raw")
+        nc.sync.dma_start(
+            out=raw[:].rearrange("p (o t) x -> p o (t x)", t=PACK),
+            in_=w2[first : first + W2_COLS].rearrange("o (p t) k i j -> p o (t k i j)", t=PACK),
+        )
+        by_row = raw[:].rearrange("p r (k i j) -> p i k r j", i=SIDE_OUT, j=SIDE_OUT)
+        for i in range(SIDE_OUT):
+            regroup(nc, SIDE_OUT * s + i, slabs[i], PIECE_ROWS * s, by_row[:, i])
+
+
+def quantise_w2_half(nc, slabs, w_words, w_planes, half):
+    for window in WINDOWS:
+        for i, j in positions_of(window):
+            for k in range(OFFSETS):
+                quantise_half_operand(nc, slabs[i], w_words[i], w_planes[i], SIDE_OUT * k + j, half)
+
+
+def load_and_quantise_h(nc, raw_pool, h_pool1, slabs, h_words, h_planes):
+    pieces = H_COLS * PACK // PIECE_ROWS
+    for half in range(BATCH // HALF):
+        for s in range(HALF // H_COLS):
+            first = half * HALF + s * H_COLS
+            raw = raw_pool.tile([P, H_COLS * PACK, SIDE_IN * SIDE_IN], BF16, tag="raw")
+            nc.sync.dma_start(
+                out=raw[:].rearrange("p (n t) x -> p n (t x)", t=PACK),
+                in_=h_pool1[first : first + H_COLS].rearrange("n (p t) r s -> p n (t r s)", t=PACK),
+            )
+            for q in range(pieces):
+                raw_rows = raw[:, q * PIECE_ROWS : (q + 1) * PIECE_ROWS, :]
+                regroup(
+                    nc,
+                    pieces * s + q,
+                    slabs[half],
+                    (pieces * s + q) * PIECE_ROWS,
+                    raw_rows.rearrange("p r (a b) -> p a r b", b=RUN),
+                )
+        for pixel in range(SHELF):
+            quantise_half_operand(nc, slabs[half], h_words, h_planes, pixel, half)
+
+
+def tile_locallyconnectednet_pa_kernel(tc, h_pool1, w2, b2, fc1_w, fc1_b, out):
+    nc = tc.nc
+    with ExitStack() as ctx:
+        ctx.enter_context(tc.manual_schedule())
+        keep = ctx.enter_context(tc.tile_pool(name="keep", bufs=1))
+        psum = ctx.enter_context(tc.psum_pool(name="psum", bufs=4))
+
+        shelves = range(SIDE_OUT)
+        w_words = [keep.tile([P, SHELF, OUT_CH], U32, name="w_words%d" % i, align_bytes=64) for i in shelves]
+        w_planes = [keep.tile([P, SHELF, OUT_CH], U8, name="w_planes%d" % i, align_bytes=64) for i in shelves]
+        slabs = [keep.tile([P, SHELF, HALF * PACK], BF16, name="slab%d" % i, align_bytes=64) for i in shelves]
+        h_words = keep.tile([P, SHELF, BATCH], U32, align_bytes=64)
+        h_planes = keep.tile([P, SHELF, BATCH], U8, align_bytes=64)
+
+        b2_bf16 = keep.tile([P, SIDE_OUT * SIDE_OUT], BF16)
+        nc.scalar.dma_start(out=b2_bf16[:], in_=b2.rearrange("o i j -> o (i j)"))
+        dense_bias = keep.tile([P, DENSE_OUT], BF16)
+        nc.scalar.dma_start(out=dense_bias[:], in_=fc1_b.partition_broadcast(P))
+
+        dense_raw = keep.tile([P, PACK, DENSE_OUT], BF16)
+        nc.sync.dma_start(out=dense_raw[:], in_=fc1_w.rearrange("(p t) f -> p t f", t=PACK))
+        dense_grouped = keep.tile([P, DENSE_OUT, PACK], BF16, align_bytes=64)
+        nc.vector.tensor_copy(
+            out=dense_grouped[:].rearrange("p (c b) t -> p c t b", b=RUN),
+            in_=dense_raw[:].rearrange("p t (c b) -> p c t b", b=RUN),
+        )
+        b2_f32 = keep.tile([P, SIDE_OUT * SIDE_OUT], F32)
+        nc.vector.tensor_copy(out=b2_f32[:], in_=b2_bf16[:])
+        dense_words = keep.tile([P, DENSE_OUT], U32, align_bytes=64)
+        dense_planes = keep.tile([P, DENSE_OUT], U8, align_bytes=64)
+        nc.vector.quantize_mx(
+            out=dense_words[:].bitcast(FP8X4),
+            scales=dense_planes[:],
+            in_=dense_grouped[:].rearrange("p f t -> p (f t)"),
+        )
+
+        with tc.tile_pool(name="raw", bufs=4) as raw_pool:
+            load_w2_half(nc, raw_pool, w2, slabs, 0)
+            quantise_w2_half(nc, slabs, w_words, w_planes, 0)
+            load_and_quantise_h(nc, raw_pool, h_pool1, slabs, h_words, h_planes)
+            load_w2_half(nc, raw_pool, w2, slabs, 1)
+        quantise_w2_half(nc, slabs, w_words, w_planes, 1)
+
+        tail = ctx.enter_context(tc.tile_pool(name="tail", bufs=1))
+        g_grouped = tail.tile([P, BATCH, PACK], BF16, align_bytes=64)
+        for w, window in enumerate(WINDOWS):
+            relu_maps = tail.tile([P, POOL * POOL, BATCH], F32, bufs=len(WINDOWS))
+            for a, (i, j) in enumerate(positions_of(window)):
+                acc = psum.tile([P, BATCH], F32)
+                for k in range(OFFSETS):
+                    di, dj = divmod(k, KS)
+                    pixel = (i + di) * SIDE_IN + j + dj
+                    operand = SIDE_OUT * k + j
+                    nc.tensor.matmul_mx(
+                        out=acc[:],
+                        lhsT=w_words[i][:, operand, :].bitcast(FP8X4),
+                        lhsT_scale=w_planes[i][:, operand, :],
+                        rhs=h_words[:, pixel, :].bitcast(FP8X4),
+                        rhs_scale=h_planes[:, pixel, :],
+                        start=(k == 0),
+                        stop=(k == OFFSETS - 1),
+                    )
+                position = SIDE_OUT * i + j
+                nc.scalar.activation(
+                    out=relu_maps[:, a, :],
+                    in_=acc[:],
+                    func=RELU,
+                    bias=b2_f32[:, position : position + 1],
+                    scale=1.0,
+                )
+            pair_max = tail.tile([P, POOL, BATCH], F32, bufs=2)
+            nc.vector.tensor_max(out=pair_max[:], in0=relu_maps[:, 0:POOL, :], in1=relu_maps[:, POOL:, :])
+            nc.vector.tensor_max(out=g_grouped[:, :, w], in0=pair_max[:, 0, :], in1=pair_max[:, 1, :])
+
+        g_words = tail.tile([P, BATCH], U32, align_bytes=64)
+        g_planes = tail.tile([P, BATCH], U8, align_bytes=64)
+        nc.vector.quantize_mx(
+            out=g_words[:].bitcast(FP8X4),
+            scales=g_planes[:],
+            in_=g_grouped[:].rearrange("p n t -> p (n t)"),
+        )
+        dense_acc = psum.tile([P, DENSE_OUT], F32, bufs=1)
+        nc.tensor.matmul_mx(
+            out=dense_acc[:],
+            lhsT=g_words[:].bitcast(FP8X4),
+            lhsT_scale=g_planes[:],
+            rhs=dense_words[:].bitcast(FP8X4),
+            rhs_scale=dense_planes[:],
+            start=True,
+            stop=True,
+        )
+        result = tail.tile([P, DENSE_OUT], F32)
+        nc.vector.tensor_add(out=result[:], in0=dense_acc[:], in1=dense_bias[:])
+        nc.vector.tensor_relu(out=result[:], in_=result[:])
+        nc.sync.dma_start(out=out, in_=result[:])

@@ -117,8 +117,6 @@ def tile_locallyconnectednet_pa_kernel(tc, h_pool1, w2, b2, fc1_w, fc1_b, out):
 
         b2_bf16 = keep.tile([P, SIDE_OUT * SIDE_OUT], BF16)
         nc.scalar.dma_start(out=b2_bf16[:], in_=b2.rearrange("o i j -> o (i j)"))
-        dense_bias = keep.tile([P, DENSE_OUT], BF16)
-        nc.scalar.dma_start(out=dense_bias[:], in_=fc1_b.partition_broadcast(P))
 
         dense_raw = keep.tile([P, PACK, DENSE_OUT], BF16)
         nc.sync.dma_start(out=dense_raw[:], in_=fc1_w.rearrange("(p t) f -> p t f", t=PACK))
@@ -142,6 +140,8 @@ def tile_locallyconnectednet_pa_kernel(tc, h_pool1, w2, b2, fc1_w, fc1_b, out):
             quantise_w2_half(nc, slabs, w_words, w_planes, 0)
             load_and_quantise_h(nc, raw_pool, h_pool1, slabs, h_words, h_planes)
             load_w2_half(nc, raw_pool, w2, slabs, 1)
+        dense_bias = keep.tile([P, DENSE_OUT], BF16)
+        nc.sync.dma_start(out=dense_bias[:], in_=fc1_b.partition_broadcast(P))
         quantise_w2_half(nc, slabs, w_words, w_planes, 1)
 
         tail = ctx.enter_context(tc.tile_pool(name="tail", bufs=1))

@@ -28,8 +28,7 @@ RAW_ELEMS = 4608
 W2_COLS = RAW_ELEMS // (PACK * OFFSETS * SIDE_OUT * SIDE_OUT)
 H_COLS = RAW_ELEMS // (PACK * SIDE_IN * SIDE_IN)
 
-VECTOR_PIECES = 3
-SCALAR_PIECES = 2
+PIECES = 4
 
 WINDOWS = [(u, v) for u in range(SIDE_OUT // POOL) for v in range(SIDE_OUT // POOL)]
 
@@ -41,9 +40,10 @@ def positions_of(window):
     return [(POOL * u + a, POOL * v + b) for a in range(POOL) for b in range(POOL)]
 
 
-def regroup(nc, piece, slab, first_row, src):
+def regroup(nc, raw_index, piece, slab, first_row, src):
     dst = slab[:, :, first_row : first_row + PIECE_ROWS].rearrange("p (a b) r -> p a r b", b=RUN)
-    if piece % (VECTOR_PIECES + SCALAR_PIECES) < VECTOR_PIECES:
+    scalar_pieces = 1 + raw_index % 2
+    if piece < PIECES - scalar_pieces:
         nc.vector.tensor_copy(out=dst, in_=src)
     else:
         nc.scalar.copy(out=dst, in_=src)
@@ -68,7 +68,7 @@ def load_w2_half(nc, raw_pool, w2, slabs, half):
         )
         by_row = raw[:].rearrange("p r (k i j) -> p i k r j", i=SIDE_OUT, j=SIDE_OUT)
         for i in range(SIDE_OUT):
-            regroup(nc, SIDE_OUT * s + i, slabs[i], PIECE_ROWS * s, by_row[:, i])
+            regroup(nc, s, i, slabs[i], PIECE_ROWS * s, by_row[:, i])
 
 
 def quantise_w2_half(nc, slabs, w_words, w_planes, half):
@@ -79,7 +79,6 @@ def quantise_w2_half(nc, slabs, w_words, w_planes, half):
 
 
 def load_and_quantise_h(nc, raw_pool, h_pool1, slabs, h_words, h_planes):
-    pieces = H_COLS * PACK // PIECE_ROWS
     for half in range(BATCH // HALF):
         for s in range(HALF // H_COLS):
             first = half * HALF + s * H_COLS
@@ -88,13 +87,14 @@ def load_and_quantise_h(nc, raw_pool, h_pool1, slabs, h_words, h_planes):
                 out=raw[:].rearrange("p (n t) x -> p n (t x)", t=PACK),
                 in_=h_pool1[first : first + H_COLS].rearrange("n (p t) r s -> p n (t r s)", t=PACK),
             )
-            for q in range(pieces):
+            for q in range(PIECES):
                 raw_rows = raw[:, q * PIECE_ROWS : (q + 1) * PIECE_ROWS, :]
                 regroup(
                     nc,
-                    pieces * s + q,
+                    s,
+                    q,
                     slabs[half],
-                    (pieces * s + q) * PIECE_ROWS,
+                    (PIECES * s + q) * PIECE_ROWS,
                     raw_rows.rearrange("p r (a b) -> p a r b", b=RUN),
                 )
         for pixel in range(SHELF):
@@ -115,18 +115,28 @@ def tile_locallyconnectednet_pa_kernel(tc, h_pool1, w2, b2, fc1_w, fc1_b, out):
         h_words = keep.tile([P, SHELF, BATCH], U32, align_bytes=64)
         h_planes = keep.tile([P, SHELF, BATCH], U8, align_bytes=64)
 
-        b2_bf16 = keep.tile([P, SIDE_OUT * SIDE_OUT], BF16)
-        nc.scalar.dma_start(out=b2_bf16[:], in_=b2.rearrange("o i j -> o (i j)"))
+        with tc.tile_pool(name="raw", bufs=4) as raw_pool:
+            load_w2_half(nc, raw_pool, w2, slabs, 0)
+            quantise_w2_half(nc, slabs, w_words, w_planes, 0)
+            load_and_quantise_h(nc, raw_pool, h_pool1, slabs, h_words, h_planes)
+            load_w2_half(nc, raw_pool, w2, slabs, 1)
 
+        b2_bf16 = keep.tile([P, SIDE_OUT * SIDE_OUT], BF16)
+        nc.sync.dma_start(out=b2_bf16[:], in_=b2.rearrange("o i j -> o (i j)"))
         dense_raw = keep.tile([P, PACK, DENSE_OUT], BF16)
         nc.sync.dma_start(out=dense_raw[:], in_=fc1_w.rearrange("(p t) f -> p t f", t=PACK))
+        dense_bias = keep.tile([P, DENSE_OUT], BF16)
+        nc.sync.dma_start(out=dense_bias[:], in_=fc1_b.partition_broadcast(P))
+
+        b2_f32 = keep.tile([P, SIDE_OUT * SIDE_OUT], F32)
+        nc.scalar.copy(out=b2_f32[:], in_=b2_bf16[:])
         dense_grouped = keep.tile([P, DENSE_OUT, PACK], BF16, align_bytes=64)
-        nc.vector.tensor_copy(
+        nc.scalar.copy(
             out=dense_grouped[:].rearrange("p (c b) t -> p c t b", b=RUN),
             in_=dense_raw[:].rearrange("p t (c b) -> p c t b", b=RUN),
         )
-        b2_f32 = keep.tile([P, SIDE_OUT * SIDE_OUT], F32)
-        nc.vector.tensor_copy(out=b2_f32[:], in_=b2_bf16[:])
+
+        quantise_w2_half(nc, slabs, w_words, w_planes, 1)
         dense_words = keep.tile([P, DENSE_OUT], U32, align_bytes=64)
         dense_planes = keep.tile([P, DENSE_OUT], U8, align_bytes=64)
         nc.vector.quantize_mx(
@@ -134,15 +144,6 @@ def tile_locallyconnectednet_pa_kernel(tc, h_pool1, w2, b2, fc1_w, fc1_b, out):
             scales=dense_planes[:],
             in_=dense_grouped[:].rearrange("p f t -> p (f t)"),
         )
-
-        with tc.tile_pool(name="raw", bufs=4) as raw_pool:
-            load_w2_half(nc, raw_pool, w2, slabs, 0)
-            quantise_w2_half(nc, slabs, w_words, w_planes, 0)
-            load_and_quantise_h(nc, raw_pool, h_pool1, slabs, h_words, h_planes)
-            load_w2_half(nc, raw_pool, w2, slabs, 1)
-        dense_bias = keep.tile([P, DENSE_OUT], BF16)
-        nc.sync.dma_start(out=dense_bias[:], in_=fc1_b.partition_broadcast(P))
-        quantise_w2_half(nc, slabs, w_words, w_planes, 1)
 
         tail = ctx.enter_context(tc.tile_pool(name="tail", bufs=1))
         g_grouped = tail.tile([P, BATCH, PACK], BF16, align_bytes=64)

@@ -42,7 +42,7 @@ def positions_of(window):
 
 def regroup(nc, raw_index, piece, slab, first_row, src):
     dst = slab[:, :, first_row : first_row + PIECE_ROWS].rearrange("p (a b) r -> p a r b", b=RUN)
-    scalar_pieces = 1 + raw_index % 2
+    scalar_pieces = 2
     if piece < PIECES - scalar_pieces:
         nc.vector.tensor_copy(out=dst, in_=src)
     else:

@@ -6,6 +6,7 @@ BF16 = mybir.dt.bfloat16
 F32 = mybir.dt.float32
 U32 = mybir.dt.uint32
 U8 = mybir.dt.uint8
+I32 = mybir.dt.int32
 FP8X4 = mybir.dt.float8_e4m3fn_x4
 RELU = mybir.ActivationFunctionType.Relu
 
@@ -78,6 +79,56 @@ def quantise_w2_half(nc, slabs, w_words, w_planes, half):
                 quantise_half_operand(nc, slabs[i], w_words[i], w_planes[i], SIDE_OUT * k + j, half)
 
 
+QUARTER = 32
+FIRST_ARRIVING = 96
+LAST_ARRIVING = 64
+
+
+def quantise_quarter_operand(nc, slab, words, planes, operand, slab_quarter, first_col):
+    width = QUARTER * PACK
+    nc.vector.quantize_mx(
+        out=words[:, operand, first_col : first_col + QUARTER].bitcast(FP8X4),
+        scales=planes[:, operand, LAST_ARRIVING : LAST_ARRIVING + QUARTER],
+        in_=slab[:, operand, slab_quarter * width : (slab_quarter + 1) * width],
+    )
+
+
+def move_scales(nc, planes):
+    nc.vector.tensor_copy(
+        out=planes[:, :, FIRST_ARRIVING : FIRST_ARRIVING + QUARTER].bitcast(I32),
+        in_=planes[:, :, LAST_ARRIVING : LAST_ARRIVING + QUARTER].bitcast(I32),
+    )
+
+
+def load_second_half(nc, raw_pool, w2, slabs, w_words, w_planes):
+    tiles = QUARTER // W2_COLS
+    for s in range(2 * tiles):
+        first = FIRST_ARRIVING + s * W2_COLS if s < tiles else LAST_ARRIVING + (s - tiles) * W2_COLS
+        raw = raw_pool.tile([P, W2_COLS * PACK, OFFSETS * SIDE_OUT * SIDE_OUT], BF16, tag="raw")
+        nc.sync.dma_start(
+            out=raw[:].rearrange("p (o t) x -> p o (t x)", t=PACK),
+            in_=w2[first : first + W2_COLS].rearrange("o (p t) k i j -> p o (t k i j)", t=PACK),
+        )
+        if s >= tiles:
+            shelf = s - tiles
+            for operand in range(SHELF):
+                quantise_quarter_operand(nc, slabs[shelf], w_words[shelf], w_planes[shelf], operand, 0, FIRST_ARRIVING)
+            if shelf > 0:
+                move_scales(nc, w_planes[shelf - 1])
+            if shelf == SIDE_OUT - 1:
+                move_scales(nc, w_planes[shelf])
+        by_row = raw[:].rearrange("p r (k i j) -> p i k r j", i=SIDE_OUT, j=SIDE_OUT)
+        for i in range(SIDE_OUT):
+            regroup(nc, s, i, slabs[i], PIECE_ROWS * s, by_row[:, i])
+
+
+def quantise_last_quarter(nc, slabs, w_words, w_planes):
+    for window in WINDOWS:
+        for i, j in positions_of(window):
+            for k in range(OFFSETS):
+                quantise_quarter_operand(nc, slabs[i], w_words[i], w_planes[i], SIDE_OUT * k + j, 1, LAST_ARRIVING)
+
+
 def load_and_quantise_h(nc, raw_pool, h_pool1, slabs, h_words, h_planes):
     for half in range(BATCH // HALF):
         for s in range(HALF // H_COLS):
@@ -115,11 +166,14 @@ def tile_locallyconnectednet_pa_kernel(tc, h_pool1, w2, b2, fc1_w, fc1_b, out):
         h_words = keep.tile([P, SHELF, BATCH], U32, align_bytes=64)
         h_planes = keep.tile([P, SHELF, BATCH], U8, align_bytes=64)
 
+        for i in shelves:
+            nc.vector.memset(w_planes[i][:, :, LAST_ARRIVING : LAST_ARRIVING + QUARTER].bitcast(I32), 0)
+
         with tc.tile_pool(name="raw", bufs=4) as raw_pool:
             load_w2_half(nc, raw_pool, w2, slabs, 0)
             quantise_w2_half(nc, slabs, w_words, w_planes, 0)
             load_and_quantise_h(nc, raw_pool, h_pool1, slabs, h_words, h_planes)
-            load_w2_half(nc, raw_pool, w2, slabs, 1)
+            load_second_half(nc, raw_pool, w2, slabs, w_words, w_planes)
 
         b2_bf16 = keep.tile([P, SIDE_OUT * SIDE_OUT], BF16)
         nc.sync.dma_start(out=b2_bf16[:], in_=b2.rearrange("o i j -> o (i j)"))
@@ -136,7 +190,7 @@ def tile_locallyconnectednet_pa_kernel(tc, h_pool1, w2, b2, fc1_w, fc1_b, out):
             in_=dense_raw[:].rearrange("p t (c b) -> p c t b", b=RUN),
         )
 
-        quantise_w2_half(nc, slabs, w_words, w_planes, 1)
+        quantise_last_quarter(nc, slabs, w_words, w_planes)
         dense_words = keep.tile([P, DENSE_OUT], U32, align_bytes=64)
         dense_planes = keep.tile([P, DENSE_OUT], U8, align_bytes=64)
         nc.vector.quantize_mx(

@@ -80,53 +80,57 @@ def quantise_w2_half(nc, slabs, w_words, w_planes, half):
 
 
 QUARTER = 32
-FIRST_ARRIVING = 96
-LAST_ARRIVING = 64
+UPPER = 96
+LOWER = 64
+LATE_SHELVES = (2, 3)
 
 
-def quantise_quarter_operand(nc, slab, words, planes, operand, slab_quarter, first_col):
-    width = QUARTER * PACK
+def quantise_quarter_operand(nc, slab, words, planes, operand, first_col):
+    first = (first_col - LOWER) * PACK
     nc.vector.quantize_mx(
         out=words[:, operand, first_col : first_col + QUARTER].bitcast(FP8X4),
-        scales=planes[:, operand, LAST_ARRIVING : LAST_ARRIVING + QUARTER],
-        in_=slab[:, operand, slab_quarter * width : (slab_quarter + 1) * width],
+        scales=planes[:, operand, LOWER : LOWER + QUARTER],
+        in_=slab[:, operand, first : first + QUARTER * PACK],
     )
 
 
 def move_scales(nc, planes):
     nc.vector.tensor_copy(
-        out=planes[:, :, FIRST_ARRIVING : FIRST_ARRIVING + QUARTER].bitcast(I32),
-        in_=planes[:, :, LAST_ARRIVING : LAST_ARRIVING + QUARTER].bitcast(I32),
+        out=planes[:, :, UPPER : UPPER + QUARTER].bitcast(I32),
+        in_=planes[:, :, LOWER : LOWER + QUARTER].bitcast(I32),
     )
 
 
 def load_second_half(nc, raw_pool, w2, slabs, w_words, w_planes):
     tiles = QUARTER // W2_COLS
     for s in range(2 * tiles):
-        first = FIRST_ARRIVING + s * W2_COLS if s < tiles else LAST_ARRIVING + (s - tiles) * W2_COLS
+        first = UPPER + s * W2_COLS if s < tiles else LOWER + (s - tiles) * W2_COLS
         raw = raw_pool.tile([P, W2_COLS * PACK, OFFSETS * SIDE_OUT * SIDE_OUT], BF16, tag="raw")
         nc.sync.dma_start(
             out=raw[:].rearrange("p (o t) x -> p o (t x)", t=PACK),
             in_=w2[first : first + W2_COLS].rearrange("o (p t) k i j -> p o (t k i j)", t=PACK),
         )
         if s >= tiles:
-            shelf = s - tiles
-            for operand in range(SHELF):
-                quantise_quarter_operand(nc, slabs[shelf], w_words[shelf], w_planes[shelf], operand, 0, FIRST_ARRIVING)
-            if shelf > 0:
-                move_scales(nc, w_planes[shelf - 1])
-            if shelf == SIDE_OUT - 1:
-                move_scales(nc, w_planes[shelf])
+            shelf = LATE_SHELVES[(s - tiles) // 2]
+            part = (s - tiles) % 2
+            for operand in range(part * SHELF // 2, (part + 1) * SHELF // 2):
+                quantise_quarter_operand(nc, slabs[shelf], w_words[shelf], w_planes[shelf], operand, UPPER)
         by_row = raw[:].rearrange("p r (k i j) -> p i k r j", i=SIDE_OUT, j=SIDE_OUT)
         for i in range(SIDE_OUT):
-            regroup(nc, s, i, slabs[i], PIECE_ROWS * s, by_row[:, i])
+            regroup(nc, s, i, slabs[i], (first - LOWER) * PACK, by_row[:, i])
+    for shelf in LATE_SHELVES:
+        move_scales(nc, w_planes[shelf])
 
 
-def quantise_last_quarter(nc, slabs, w_words, w_planes):
+def quantise_rest(nc, slabs, w_words, w_planes):
     for window in WINDOWS:
         for i, j in positions_of(window):
             for k in range(OFFSETS):
-                quantise_quarter_operand(nc, slabs[i], w_words[i], w_planes[i], SIDE_OUT * k + j, 1, LAST_ARRIVING)
+                operand = SIDE_OUT * k + j
+                if i in LATE_SHELVES:
+                    quantise_quarter_operand(nc, slabs[i], w_words[i], w_planes[i], operand, LOWER)
+                else:
+                    quantise_half_operand(nc, slabs[i], w_words[i], w_planes[i], operand, 1)
 
 
 def load_and_quantise_h(nc, raw_pool, h_pool1, slabs, h_words, h_planes):
@@ -166,8 +170,8 @@ def tile_locallyconnectednet_pa_kernel(tc, h_pool1, w2, b2, fc1_w, fc1_b, out):
         h_words = keep.tile([P, SHELF, BATCH], U32, align_bytes=64)
         h_planes = keep.tile([P, SHELF, BATCH], U8, align_bytes=64)
 
-        for i in shelves:
-            nc.vector.memset(w_planes[i][:, :, LAST_ARRIVING : LAST_ARRIVING + QUARTER].bitcast(I32), 0)
+        for i in LATE_SHELVES:
+            nc.vector.memset(w_planes[i][:, :, LOWER : LOWER + QUARTER].bitcast(I32), 0)
 
         with tc.tile_pool(name="raw", bufs=4) as raw_pool:
             load_w2_half(nc, raw_pool, w2, slabs, 0)
@@ -190,7 +194,7 @@ def tile_locallyconnectednet_pa_kernel(tc, h_pool1, w2, b2, fc1_w, fc1_b, out):
             in_=dense_raw[:].rearrange("p t (c b) -> p c t b", b=RUN),
         )
 
-        quantise_last_quarter(nc, slabs, w_words, w_planes)
+        quantise_rest(nc, slabs, w_words, w_planes)
         dense_words = keep.tile([P, DENSE_OUT], U32, align_bytes=64)
         dense_planes = keep.tile([P, DENSE_OUT], U8, align_bytes=64)
         nc.vector.quantize_mx(

@@ -159,7 +159,6 @@ def load_and_quantise_h(nc, raw_pool, h_pool1, slabs, h_words, h_planes):
 def tile_locallyconnectednet_pa_kernel(tc, h_pool1, w2, b2, fc1_w, fc1_b, out):
     nc = tc.nc
     with ExitStack() as ctx:
-        ctx.enter_context(tc.manual_schedule())
         keep = ctx.enter_context(tc.tile_pool(name="keep", bufs=1))
         psum = ctx.enter_context(tc.psum_pool(name="psum", bufs=4))
 

from contextlib import ExitStack

import concourse.mybir as mybir

BF16 = mybir.dt.bfloat16
F32 = mybir.dt.float32
U32 = mybir.dt.uint32
U8 = mybir.dt.uint8
I32 = mybir.dt.int32
FP8X4 = mybir.dt.float8_e4m3fn_x4
RELU = mybir.ActivationFunctionType.Relu

P = 128
PACK = 4
BATCH = 128
OUT_CH = 128
SIDE_IN = 6
KS = 3
OFFSETS = KS * KS
SIDE_OUT = 4
POOL = 2
DENSE_OUT = 512

SHELF = 36
HALF = 64
RUN = 4
PIECE_ROWS = 32
RAW_ELEMS = 4608
W2_COLS = RAW_ELEMS // (PACK * OFFSETS * SIDE_OUT * SIDE_OUT)
H_COLS = RAW_ELEMS // (PACK * SIDE_IN * SIDE_IN)

PIECES = 4

WINDOWS = [(u, v) for u in range(SIDE_OUT // POOL) for v in range(SIDE_OUT // POOL)]

FLOPS = 2 * BATCH * OUT_CH * 512 * OFFSETS * SIDE_OUT * SIDE_OUT + 2 * BATCH * 512 * DENSE_OUT


def positions_of(window):
    u, v = window
    return [(POOL * u + a, POOL * v + b) for a in range(POOL) for b in range(POOL)]


def regroup(nc, raw_index, piece, slab, first_row, src):
    dst = slab[:, :, first_row : first_row + PIECE_ROWS].rearrange("p (a b) r -> p a r b", b=RUN)
    scalar_pieces = 2
    if piece < PIECES - scalar_pieces:
        nc.vector.tensor_copy(out=dst, in_=src)
    else:
        nc.scalar.copy(out=dst, in_=src)


def quantise_half_operand(nc, slab, words, planes, operand, half):
    cols = slice(half * HALF, (half + 1) * HALF)
    nc.vector.quantize_mx(
        out=words[:, operand, cols].bitcast(FP8X4),
        scales=planes[:, operand, cols],
        in_=slab[:, operand, :],
    )


def load_w2_half(nc, raw_pool, w2, slabs, half):
    for s in range(HALF // W2_COLS):
        first = half * HALF + s * W2_COLS
        raw = raw_pool.tile([P, W2_COLS * PACK, OFFSETS * SIDE_OUT * SIDE_OUT], BF16, tag="raw")
        nc.sync.dma_start(
            out=raw[:].rearrange("p (o t) x -> p o (t x)", t=PACK),
            in_=w2[first : first + W2_COLS].rearrange("o (p t) k i j -> p o (t k i j)", t=PACK),
        )
        by_row = raw[:].rearrange("p r (k i j) -> p i k r j", i=SIDE_OUT, j=SIDE_OUT)
        for i in range(SIDE_OUT):
            regroup(nc, s, i, slabs[i], PIECE_ROWS * s, by_row[:, i])


def quantise_w2_half(nc, slabs, w_words, w_planes, half):
    for window in WINDOWS:
        for i, j in positions_of(window):
            for k in range(OFFSETS):
                quantise_half_operand(nc, slabs[i], w_words[i], w_planes[i], SIDE_OUT * k + j, half)


QUARTER = 32
UPPER = 96
LOWER = 64
LATE_SHELVES = (2, 3)


def quantise_quarter_operand(nc, slab, words, planes, operand, first_col):
    first = (first_col - LOWER) * PACK
    nc.vector.quantize_mx(
        out=words[:, operand, first_col : first_col + QUARTER].bitcast(FP8X4),
        scales=planes[:, operand, LOWER : LOWER + QUARTER],
        in_=slab[:, operand, first : first + QUARTER * PACK],
    )


def move_scales(nc, planes):
    nc.vector.tensor_copy(
        out=planes[:, :, UPPER : UPPER + QUARTER].bitcast(I32),
        in_=planes[:, :, LOWER : LOWER + QUARTER].bitcast(I32),
    )


def load_second_half(nc, raw_pool, w2, slabs, w_words, w_planes):
    tiles = QUARTER // W2_COLS
    for s in range(2 * tiles):
        first = UPPER + s * W2_COLS if s < tiles else LOWER + (s - tiles) * W2_COLS
        raw = raw_pool.tile([P, W2_COLS * PACK, OFFSETS * SIDE_OUT * SIDE_OUT], BF16, tag="raw")
        nc.sync.dma_start(
            out=raw[:].rearrange("p (o t) x -> p o (t x)", t=PACK),
            in_=w2[first : first + W2_COLS].rearrange("o (p t) k i j -> p o (t k i j)", t=PACK),
        )
        if s >= tiles:
            shelf = LATE_SHELVES[(s - tiles) // 2]
            part = (s - tiles) % 2
            for operand in range(part * SHELF // 2, (part + 1) * SHELF // 2):
                quantise_quarter_operand(nc, slabs[shelf], w_words[shelf], w_planes[shelf], operand, UPPER)
        by_row = raw[:].rearrange("p r (k i j) -> p i k r j", i=SIDE_OUT, j=SIDE_OUT)
        for i in range(SIDE_OUT):
            regroup(nc, s, i, slabs[i], (first - LOWER) * PACK, by_row[:, i])
    for shelf in LATE_SHELVES:
        move_scales(nc, w_planes[shelf])


def quantise_rest(nc, slabs, w_words, w_planes):
    for window in WINDOWS:
        for i, j in positions_of(window):
            for k in range(OFFSETS):
                operand = SIDE_OUT * k + j
                if i in LATE_SHELVES:
                    quantise_quarter_operand(nc, slabs[i], w_words[i], w_planes[i], operand, LOWER)
                else:
                    quantise_half_operand(nc, slabs[i], w_words[i], w_planes[i], operand, 1)


def load_and_quantise_h(nc, raw_pool, h_pool1, slabs, h_words, h_planes):
    for half in range(BATCH // HALF):
        for s in range(HALF // H_COLS):
            first = half * HALF + s * H_COLS
            raw = raw_pool.tile([P, H_COLS * PACK, SIDE_IN * SIDE_IN], BF16, tag="raw")
            nc.sync.dma_start(
                out=raw[:].rearrange("p (n t) x -> p n (t x)", t=PACK),
                in_=h_pool1[first : first + H_COLS].rearrange("n (p t) r s -> p n (t r s)", t=PACK),
            )
            for q in range(PIECES):
                raw_rows = raw[:, q * PIECE_ROWS : (q + 1) * PIECE_ROWS, :]
                regroup(
                    nc,
                    s,
                    q,
                    slabs[half],
                    (PIECES * s + q) * PIECE_ROWS,
                    raw_rows.rearrange("p r (a b) -> p a r b", b=RUN),
                )
        for pixel in range(SHELF):
            quantise_half_operand(nc, slabs[half], h_words, h_planes, pixel, half)


def tile_locallyconnectednet_pa_kernel(tc, h_pool1, w2, b2, fc1_w, fc1_b, out):
    nc = tc.nc
    with ExitStack() as ctx:
        keep = ctx.enter_context(tc.tile_pool(name="keep", bufs=1))
        psum = ctx.enter_context(tc.psum_pool(name="psum", bufs=4))

        shelves = range(SIDE_OUT)
        w_words = [keep.tile([P, SHELF, OUT_CH], U32, name="w_words%d" % i, align_bytes=64) for i in shelves]
        w_planes = [keep.tile([P, SHELF, OUT_CH], U8, name="w_planes%d" % i, align_bytes=64) for i in shelves]
        slabs = [keep.tile([P, SHELF, HALF * PACK], BF16, name="slab%d" % i, align_bytes=64) for i in shelves]
        h_words = keep.tile([P, SHELF, BATCH], U32, align_bytes=64)
        h_planes = keep.tile([P, SHELF, BATCH], U8, align_bytes=64)

        for i in LATE_SHELVES:
            nc.vector.memset(w_planes[i][:, :, LOWER : LOWER + QUARTER].bitcast(I32), 0)

        with tc.tile_pool(name="raw", bufs=4) as raw_pool:
            load_w2_half(nc, raw_pool, w2, slabs, 0)
            quantise_w2_half(nc, slabs, w_words, w_planes, 0)
            load_and_quantise_h(nc, raw_pool, h_pool1, slabs, h_words, h_planes)
            load_second_half(nc, raw_pool, w2, slabs, w_words, w_planes)

        b2_bf16 = keep.tile([P, SIDE_OUT * SIDE_OUT], BF16)
        nc.sync.dma_start(out=b2_bf16[:], in_=b2.rearrange("o i j -> o (i j)"))
        dense_raw = keep.tile([P, PACK, DENSE_OUT], BF16)
        nc.sync.dma_start(out=dense_raw[:], in_=fc1_w.rearrange("(p t) f -> p t f", t=PACK))
        dense_bias = keep.tile([P, DENSE_OUT], BF16)
        nc.sync.dma_start(out=dense_bias[:], in_=fc1_b.partition_broadcast(P))

        b2_f32 = keep.tile([P, SIDE_OUT * SIDE_OUT], F32)
        nc.scalar.copy(out=b2_f32[:], in_=b2_bf16[:])
        dense_grouped = keep.tile([P, DENSE_OUT, PACK], BF16, align_bytes=64)
        nc.scalar.copy(
            out=dense_grouped[:].rearrange("p (c b) t -> p c t b", b=RUN),
            in_=dense_raw[:].rearrange("p t (c b) -> p c t b", b=RUN),
        )

        quantise_rest(nc, slabs, w_words, w_planes)
        dense_words = keep.tile([P, DENSE_OUT], U32, align_bytes=64)
        dense_planes = keep.tile([P, DENSE_OUT], U8, align_bytes=64)
        nc.vector.quantize_mx(
            out=dense_words[:].bitcast(FP8X4),
            scales=dense_planes[:],
            in_=dense_grouped[:].rearrange("p f t -> p (f t)"),
        )

        tail = ctx.enter_context(tc.tile_pool(name="tail", bufs=1))
        g_grouped = tail.tile([P, BATCH, PACK], BF16, align_bytes=64)
        for w, window in enumerate(WINDOWS):
            relu_maps = tail.tile([P, POOL * POOL, BATCH], F32, bufs=len(WINDOWS))
            for a, (i, j) in enumerate(positions_of(window)):
                acc = psum.tile([P, BATCH], F32)
                for k in range(OFFSETS):
                    di, dj = divmod(k, KS)
                    pixel = (i + di) * SIDE_IN + j + dj
                    operand = SIDE_OUT * k + j
                    nc.tensor.matmul_mx(
                        out=acc[:],
                        lhsT=w_words[i][:, operand, :].bitcast(FP8X4),
                        lhsT_scale=w_planes[i][:, operand, :],
                        rhs=h_words[:, pixel, :].bitcast(FP8X4),
                        rhs_scale=h_planes[:, pixel, :],
                        start=(k == 0),
                        stop=(k == OFFSETS - 1),
                    )
                position = SIDE_OUT * i + j
                nc.scalar.activation(
                    out=relu_maps[:, a, :],
                    in_=acc[:],
                    func=RELU,
                    bias=b2_f32[:, position : position + 1],
                    scale=1.0,
                )
            pair_max = tail.tile([P, POOL, BATCH], F32, bufs=2)
            nc.vector.tensor_max(out=pair_max[:], in0=relu_maps[:, 0:POOL, :], in1=relu_maps[:, POOL:, :])
            nc.vector.tensor_max(out=g_grouped[:, :, w], in0=pair_max[:, 0, :], in1=pair_max[:, 1, :])

        g_words = tail.tile([P, BATCH], U32, align_bytes=64)
        g_planes = tail.tile([P, BATCH], U8, align_bytes=64)
        nc.vector.quantize_mx(
            out=g_words[:].bitcast(FP8X4),
            scales=g_planes[:],
            in_=g_grouped[:].rearrange("p n t -> p (n t)"),
        )
        dense_acc = psum.tile([P, DENSE_OUT], F32, bufs=1)
        nc.tensor.matmul_mx(
            out=dense_acc[:],
            lhsT=g_words[:].bitcast(FP8X4),
            lhsT_scale=g_planes[:],
            rhs=dense_words[:].bitcast(FP8X4),
            rhs_scale=dense_planes[:],
            start=True,
            stop=True,
        )
        result = tail.tile([P, DENSE_OUT], F32)
        nc.vector.tensor_add(out=result[:], in0=dense_acc[:], in1=dense_bias[:])
        nc.vector.tensor_relu(out=result[:], in_=result[:])
        nc.sync.dma_start(out=out, in_=result[:])
